import numpy as np
import ml_dtypes


def mxq(x, axis, fmt="e4m3"):
    dtype, down = {"e4m3": (ml_dtypes.float8_e4m3fn, 7), "e5m2": (ml_dtypes.float8_e5m2, 14)}[fmt]
    v = np.moveaxis(np.asarray(x, np.float32).astype(ml_dtypes.bfloat16).astype(np.float64), axis, -1)
    blocks = v.reshape(v.shape[:-1] + (-1, 32))
    amax = np.abs(blocks).max(-1, keepdims=True)
    byte = np.maximum(np.where(amax > 0, np.frexp(amax)[1] - 1 + 127, 0) - down, 1)
    scale = np.exp2(byte - 127.0)
    codes = (blocks / scale).astype(np.float32).astype(dtype).astype(np.float64)
    return np.moveaxis((codes * scale).reshape(v.shape), -1, axis)


WIDE = False


def mx_kscale(k):
    if not WIDE:
        return np.ones(k)
    levels = np.array([10, -10, 5, -5, 0])
    a = np.random.permutation(np.resize(levels, k // 512 * 4)).reshape(k // 512, 4)
    idx = np.arange(k)
    return np.exp2(a[idx // 512, idx % 128 // 32])


BF16 = ml_dtypes.bfloat16


def bf(x):
    return np.asarray(x, np.float32).astype(BF16)


def f64(x):
    return np.asarray(x).astype(np.float64)


B, D, N, L = 1024, 2048, 2048, 4
BN_EPS = 1e-5


def setup_inputs():
    t = mx_kscale(D)
    return {"h_lin": bf(np.random.standard_normal((B, D)) * 0.6 + np.random.standard_normal(D) * 0.5),
            "gamma": bf(np.random.uniform(0.5, 1.5, D) * t),
            "beta": bf(np.random.standard_normal(D) * 0.2 * t),
            "w": bf(np.random.standard_normal((D, N)) / np.sqrt(D) / t[:, None]),
            "b": bf(np.random.standard_normal(N) * 0.2)}


def reference(h_lin, gamma, beta, w, b):
    z = f64(h_lin)
    mu = z.mean(0)
    var = ((z - mu) ** 2).mean(0)
    h = np.maximum((z - mu) / np.sqrt(var + BN_EPS) * f64(gamma) + f64(beta), 0.0)
    return (mxq(h, 1, "e4m3") @ mxq(f64(w), 0, "e4m3")) + f64(b)

@@ -1,0 +1,216 @@
+from contextlib import ExitStack
+
+import concourse.masks as masks
+import concourse.mybir as mybir
+
+F32 = mybir.dt.float32
+BF16 = mybir.dt.bfloat16
+U32 = mybir.dt.uint32
+U8 = mybir.dt.uint8
+FP8X4 = mybir.dt.float8_e4m3fn_x4
+ACT = mybir.ActivationFunctionType
+ALU = mybir.AluOpType
+
+P = 128
+PACK = 4
+K_PASS = P * PACK
+N_TILE = 512
+MEAN_COLS = 32
+BN_EPS = 1e-5
+
+BATCH, D_IN, D_OUT = 1024, 2048, 2048
+FLOPS = 2 * BATCH * D_IN * D_OUT
+
+ROW_BLOCKS = BATCH // P
+PASSES = D_IN // K_PASS
+FEATURE_BLOCKS = D_IN // P
+OUT_CHUNKS = D_OUT // N_TILE
+
+
+def tile_customnetwork_pa_kernel(tc, h_lin, gamma, beta, w, b, out):
+    nc = tc.nc
+    with ExitStack() as ctx:
+        const = ctx.enter_context(tc.tile_pool(name="const", bufs=1))
+        keep = ctx.enter_context(tc.tile_pool(name="keep", bufs=1))
+        h_stage = ctx.enter_context(tc.tile_pool(name="h_stage", bufs=2))
+        squares = ctx.enter_context(tc.tile_pool(name="squares", bufs=4))
+        w_stage = ctx.enter_context(tc.tile_pool(name="w_stage", bufs=4))
+        out_stage = ctx.enter_context(tc.tile_pool(name="out_stage", bufs=6))
+        mean_bank = ctx.enter_context(tc.psum_pool(name="mean_bank", bufs=1))
+        banks = ctx.enter_context(tc.psum_pool(name="banks", bufs=7))
+
+        x_sb = []
+        for g in range(PASSES):
+            x_g = keep.tile([P, ROW_BLOCKS, K_PASS], BF16, name="x%d" % g)
+            nc.sync.dma_start(
+                out=x_g[:],
+                in_=h_lin[:, g * K_PASS : (g + 1) * K_PASS].rearrange("(r p) d -> p r d", p=P),
+            )
+            x_sb.append(x_g)
+        w_raw = []
+        for c in range(OUT_CHUNKS):
+            w_c = keep.tile([P, FEATURE_BLOCKS, N_TILE], BF16, name="w_raw%d" % c)
+            nc.sync.dma_start(
+                out=w_c[:],
+                in_=w[:, c * N_TILE : (c + 1) * N_TILE].rearrange("(j p) n -> p j n", p=P),
+            )
+            w_raw.append(w_c)
+        bias_all = const.tile([P, D_OUT], BF16)
+        nc.sync.dma_start(out=bias_all[:], in_=b.partition_broadcast(P))
+
+        ident = const.tile([P, P], BF16)
+        masks.make_identity(nc, ident[:])
+        minus_inv_batch = const.tile([P, MEAN_COLS], BF16)
+        nc.vector.memset(minus_inv_batch[:], -1.0 / BATCH)
+        eps = const.tile([P, 1], F32)
+        nc.vector.memset(eps[:], BN_EPS)
+        table_warmer = const.tile([P, 1], F32)
+        nc.scalar.activation(out=table_warmer[:], in_=eps[:], func=ACT.Sqrt)
+
+        gb_rows = const.tile([P, P], BF16)
+        nc.vector.memset(gb_rows[:], 0.0)
+        nc.scalar.dma_start(
+            out=gb_rows[0:FEATURE_BLOCKS, :], in_=gamma.rearrange("(j p) -> j p", p=P)
+        )
+        nc.scalar.dma_start(
+            out=gb_rows[FEATURE_BLOCKS : 2 * FEATURE_BLOCKS, :],
+            in_=beta.rearrange("(j p) -> j p", p=P),
+        )
+        gb_ps = banks.tile([P, P], BF16, tag="bank")
+        nc.tensor.transpose(gb_ps[:], gb_rows[:], ident[:])
+        gb_cols = const.tile([P, 2 * FEATURE_BLOCKS], F32)
+        nc.vector.tensor_copy(out=gb_cols[:], in_=gb_ps[:, 0 : 2 * FEATURE_BLOCKS])
+        gamma_cols = gb_cols[:, 0:FEATURE_BLOCKS]
+        beta_cols = gb_cols[:, FEATURE_BLOCKS : 2 * FEATURE_BLOCKS]
+
+        neg_mean_ps = mean_bank.tile([P, FEATURE_BLOCKS, MEAN_COLS], F32)
+        neg_mean = const.tile([P, FEATURE_BLOCKS], F32)
+        sum_sq = const.tile([P, FEATURE_BLOCKS], F32)
+        std = const.tile([P, FEATURE_BLOCKS], F32)
+        rstd = const.tile([P, FEATURE_BLOCKS], F32)
+        slope = const.tile([P, FEATURE_BLOCKS], F32)
+        neg_mean_slope = const.tile([P, FEATURE_BLOCKS], F32)
+        shift = const.tile([P, FEATURE_BLOCKS], F32)
+
+        h_codes = []
+        h_scales = []
+        for g in range(PASSES):
+            blocks = slice(g * PACK, (g + 1) * PACK)
+
+            for t in range(PACK):
+                for r in range(ROW_BLOCKS):
+                    nc.tensor.matmul(
+                        out=neg_mean_ps[:, g * PACK + t, :],
+                        lhsT=x_sb[g][:, r, t * P : (t + 1) * P],
+                        rhs=minus_inv_batch[:],
+                        start=(r == 0),
+                        stop=(r == ROW_BLOCKS - 1),
+                    )
+            nc.vector.tensor_copy(out=neg_mean[:, blocks], in_=neg_mean_ps[:, blocks, 0])
+
+            x_t = []
+            for t in range(PACK):
+                x_t_block = banks.tile([P, BATCH], BF16, tag="bank", name="x_t%d" % t)
+                for r in range(ROW_BLOCKS):
+                    nc.tensor.transpose(
+                        x_t_block[:, r * P : (r + 1) * P],
+                        x_sb[g][:, r, t * P : (t + 1) * P],
+                        ident[:],
+                    )
+                x_t.append(x_t_block)
+                dropped = squares.tile([P, BATCH], BF16)
+                j = g * PACK + t
+                nc.scalar.activation(
+                    out=dropped[:],
+                    in_=x_t_block[:],
+                    func=ACT.Square,
+                    bias=neg_mean[:, j : j + 1],
+                    accum_out=sum_sq[:, j : j + 1],
+                )
+
+            nc.scalar.activation(
+                out=std[:, blocks], in_=sum_sq[:, blocks], func=ACT.Sqrt,
+                bias=eps[:, 0:1], scale=1.0 / BATCH,
+            )
+            nc.vector.reciprocal(out=rstd[:, blocks], in_=std[:, blocks])
+            nc.vector.tensor_mul(out=slope[:, blocks], in0=gamma_cols[:, blocks], in1=rstd[:, blocks])
+            nc.vector.tensor_mul(
+                out=neg_mean_slope[:, blocks], in0=neg_mean[:, blocks], in1=slope[:, blocks]
+            )
+            nc.vector.tensor_add(
+                out=shift[:, blocks], in0=neg_mean_slope[:, blocks], in1=beta_cols[:, blocks]
+            )
+
+            normed = h_stage.tile([P, PACK, BATCH], BF16)
+            for t in range(PACK):
+                j = g * PACK + t
+                nc.vector.tensor_scalar(
+                    out=normed[:, t, :],
+                    in0=x_t[t][:],
+                    scalar1=slope[:, j : j + 1],
+                    scalar2=shift[:, j : j + 1],
+                    op0=ALU.mult,
+                    op1=ALU.add,
+                )
+            grouped = h_stage.tile([P, BATCH, PACK], BF16, align_bytes=64)
+            nc.vector.tensor_scalar_max(
+                out=grouped[:].rearrange("p (c i) t -> p c t i", i=4),
+                in0=normed[:].rearrange("p t (c i) -> p c t i", i=4),
+                scalar1=0.0,
+            )
+            codes = keep.tile([P, BATCH], U32, name="h_codes%d" % g, align_bytes=64)
+            scales = keep.tile([P, BATCH], U8, name="h_scales%d" % g, align_bytes=64)
+            nc.vector.quantize_mx(
+                out=codes[:].bitcast(FP8X4),
+                scales=scales[:],
+                in_=grouped[:].rearrange("p r t -> p (r t)"),
+            )
+            h_codes.append(codes)
+            h_scales.append(scales)
+
+        def quantise_w_chunk(c):
+            chunk_codes = []
+            chunk_scales = []
+            for g in range(PASSES):
+                grouped = w_stage.tile([P, N_TILE, PACK], BF16, align_bytes=64, name="w_grouped")
+                nc.scalar.copy(
+                    out=grouped[:].rearrange("p (c i) t -> p c t i", i=4),
+                    in_=w_raw[c][:, g * PACK : (g + 1) * PACK, :].rearrange(
+                        "p t (c i) -> p c t i", i=4
+                    ),
+                )
+                codes = keep.tile([P, N_TILE], U32, name="w_codes%d_%d" % (c, g), align_bytes=64)
+                scales = keep.tile([P, N_TILE], U8, name="w_scales%d_%d" % (c, g), align_bytes=64)
+                nc.vector.quantize_mx(
+                    out=codes[:].bitcast(FP8X4),
+                    scales=scales[:],
+                    in_=grouped[:].rearrange("p n t -> p (n t)"),
+                )
+                chunk_codes.append(codes)
+                chunk_scales.append(scales)
+            return chunk_codes, chunk_scales
+
+        w_next = quantise_w_chunk(0)
+        for c in range(OUT_CHUNKS):
+            w_codes, w_scales = w_next
+            if c + 1 < OUT_CHUNKS:
+                w_next = quantise_w_chunk(c + 1)
+            n_cols = slice(c * N_TILE, (c + 1) * N_TILE)
+            for m in range(ROW_BLOCKS):
+                m_cols = slice(m * P, (m + 1) * P)
+                acc = banks.tile([P, N_TILE], F32, tag="bank")
+                for g in range(PASSES):
+                    nc.tensor.matmul_mx(
+                        out=acc[:],
+                        lhsT=h_codes[g][:, m_cols].bitcast(FP8X4),
+                        lhsT_scale=h_scales[g][:, m_cols],
+                        rhs=w_codes[g][:].bitcast(FP8X4),
+                        rhs_scale=w_scales[g][:],
+                        start=(g == 0),
+                        stop=(g == PASSES - 1),
+                    )
+                result = out_stage.tile([P, N_TILE], F32)
+                nc.vector.tensor_tensor(
+                    out=result[:], in0=acc[:], in1=bias_all[:, n_cols], op=ALU.add
+                )
+                nc.sync.dma_start(out=out[m_cols, n_cols], in_=result[:])

@@ -25,38 +25,70 @@ ROW_BLOCKS = BATCH // P
 PASSES = D_IN // K_PASS
 FEATURE_BLOCKS = D_IN // P
 OUT_CHUNKS = D_OUT // N_TILE
+HALVES = 2
+HALF_BATCH = BATCH // HALVES
+HALF_PASSES = PASSES // HALVES
+SCALAR_NORM_BLOCK = PACK - 1
 
 
 def tile_customnetwork_pa_kernel(tc, h_lin, gamma, beta, w, b, out):
     nc = tc.nc
     with ExitStack() as ctx:
+        ctx.enter_context(tc.manual_schedule())
         const = ctx.enter_context(tc.tile_pool(name="const", bufs=1))
         keep = ctx.enter_context(tc.tile_pool(name="keep", bufs=1))
-        h_stage = ctx.enter_context(tc.tile_pool(name="h_stage", bufs=2))
+        normed_pool = ctx.enter_context(tc.tile_pool(name="normed_pool", bufs=2))
         squares = ctx.enter_context(tc.tile_pool(name="squares", bufs=4))
-        w_stage = ctx.enter_context(tc.tile_pool(name="w_stage", bufs=4))
+        grouped_pool = ctx.enter_context(tc.tile_pool(name="grouped_pool", bufs=4))
         out_stage = ctx.enter_context(tc.tile_pool(name="out_stage", bufs=6))
         mean_bank = ctx.enter_context(tc.psum_pool(name="mean_bank", bufs=1))
         banks = ctx.enter_context(tc.psum_pool(name="banks", bufs=7))
 
-        x_sb = []
-        for g in range(PASSES):
-            x_g = keep.tile([P, ROW_BLOCKS, K_PASS], BF16, name="x%d" % g)
+        x_sb = [
+            keep.tile([P, ROW_BLOCKS, K_PASS], BF16, name="x%d" % g) for g in range(PASSES)
+        ]
+        w_raw = [
+            [
+                keep.tile([P, HALF_PASSES * PACK, N_TILE], BF16, name="w_raw%d_%d" % (c, half))
+                for half in range(HALVES)
+            ]
+            for c in range(OUT_CHUNKS)
+        ]
+        bias_all = const.tile([P, D_OUT], BF16)
+
+        def load_x(g):
             nc.sync.dma_start(
-                out=x_g[:],
+                out=x_sb[g][:],
                 in_=h_lin[:, g * K_PASS : (g + 1) * K_PASS].rearrange("(r p) d -> p r d", p=P),
             )
-            x_sb.append(x_g)
-        w_raw = []
-        for c in range(OUT_CHUNKS):
-            w_c = keep.tile([P, FEATURE_BLOCKS, N_TILE], BF16, name="w_raw%d" % c)
+
+        def load_w(c, half):
+            rows = slice(half * HALF_PASSES * K_PASS, (half + 1) * HALF_PASSES * K_PASS)
             nc.sync.dma_start(
-                out=w_c[:],
-                in_=w[:, c * N_TILE : (c + 1) * N_TILE].rearrange("(j p) n -> p j n", p=P),
+                out=w_raw[c][half][:],
+                in_=w[rows, c * N_TILE : (c + 1) * N_TILE].rearrange("(j p) n -> p j n", p=P),
             )
-            w_raw.append(w_c)
-        bias_all = const.tile([P, D_OUT], BF16)
+
+        gb_rows = const.tile([P, P], BF16)
+        nc.sync.dma_start(
+            out=gb_rows[0:FEATURE_BLOCKS, :], in_=gamma.rearrange("(j p) -> j p", p=P)
+        )
+        nc.sync.dma_start(
+            out=gb_rows[FEATURE_BLOCKS : 2 * FEATURE_BLOCKS, :],
+            in_=beta.rearrange("(j p) -> j p", p=P),
+        )
+        nc.vector.memset(gb_rows[32:64, :], 0.0)
+        nc.vector.memset(gb_rows[64:128, :], 0.0)
+        load_x(0)
+        load_w(0, 0)
+        load_x(1)
+        load_w(0, 1)
+        load_x(2)
+        load_x(3)
         nc.sync.dma_start(out=bias_all[:], in_=b.partition_broadcast(P))
+        for c in range(1, OUT_CHUNKS):
+            for half in range(HALVES):
+                load_w(c, half)
 
         ident = const.tile([P, P], BF16)
         masks.make_identity(nc, ident[:])
@@ -66,22 +98,10 @@ def tile_customnetwork_pa_kernel(tc, h_lin, gamma, beta, w, b, out):
         nc.vector.memset(eps[:], BN_EPS)
         table_warmer = const.tile([P, 1], F32)
         nc.scalar.activation(out=table_warmer[:], in_=eps[:], func=ACT.Sqrt)
-
-        gb_rows = const.tile([P, P], BF16)
-        nc.vector.memset(gb_rows[:], 0.0)
-        nc.scalar.dma_start(
-            out=gb_rows[0:FEATURE_BLOCKS, :], in_=gamma.rearrange("(j p) -> j p", p=P)
-        )
-        nc.scalar.dma_start(
-            out=gb_rows[FEATURE_BLOCKS : 2 * FEATURE_BLOCKS, :],
-            in_=beta.rearrange("(j p) -> j p", p=P),
-        )
         gb_ps = banks.tile([P, P], BF16, tag="bank")
         nc.tensor.transpose(gb_ps[:], gb_rows[:], ident[:])
         gb_cols = const.tile([P, 2 * FEATURE_BLOCKS], F32)
         nc.vector.tensor_copy(out=gb_cols[:], in_=gb_ps[:, 0 : 2 * FEATURE_BLOCKS])
-        gamma_cols = gb_cols[:, 0:FEATURE_BLOCKS]
-        beta_cols = gb_cols[:, FEATURE_BLOCKS : 2 * FEATURE_BLOCKS]
 
         neg_mean_ps = mean_bank.tile([P, FEATURE_BLOCKS, MEAN_COLS], F32)
         neg_mean = const.tile([P, FEATURE_BLOCKS], F32)
@@ -92,11 +112,7 @@ def tile_customnetwork_pa_kernel(tc, h_lin, gamma, beta, w, b, out):
         neg_mean_slope = const.tile([P, FEATURE_BLOCKS], F32)
         shift = const.tile([P, FEATURE_BLOCKS], F32)
 
-        h_codes = []
-        h_scales = []
-        for g in range(PASSES):
-            blocks = slice(g * PACK, (g + 1) * PACK)
-
+        def means(g):
             for t in range(PACK):
                 for r in range(ROW_BLOCKS):
                     nc.tensor.matmul(
@@ -106,106 +122,143 @@ def tile_customnetwork_pa_kernel(tc, h_lin, gamma, beta, w, b, out):
                         start=(r == 0),
                         stop=(r == ROW_BLOCKS - 1),
                     )
-            nc.vector.tensor_copy(out=neg_mean[:, blocks], in_=neg_mean_ps[:, blocks, 0])
+            blocks = slice(g * PACK, (g + 1) * PACK)
+            nc.scalar.copy(out=neg_mean[:, blocks], in_=neg_mean_ps[:, blocks, 0])
 
-            x_t = []
-            for t in range(PACK):
-                x_t_block = banks.tile([P, BATCH], BF16, tag="bank", name="x_t%d" % t)
-                for r in range(ROW_BLOCKS):
-                    nc.tensor.transpose(
-                        x_t_block[:, r * P : (r + 1) * P],
-                        x_sb[g][:, r, t * P : (t + 1) * P],
-                        ident[:],
-                    )
-                x_t.append(x_t_block)
-                dropped = squares.tile([P, BATCH], BF16)
-                j = g * PACK + t
-                nc.scalar.activation(
-                    out=dropped[:],
-                    in_=x_t_block[:],
-                    func=ACT.Square,
-                    bias=neg_mean[:, j : j + 1],
-                    accum_out=sum_sq[:, j : j + 1],
+        def transpose_and_square(g, t):
+            j = g * PACK + t
+            x_t_block = banks.tile([P, BATCH], BF16, tag="bank", name="x_t")
+            for r in range(ROW_BLOCKS):
+                nc.tensor.transpose(
+                    x_t_block[:, r * P : (r + 1) * P],
+                    x_sb[g][:, r, t * P : (t + 1) * P],
+                    ident[:],
                 )
+            dropped = squares.tile([P, BATCH], BF16)
+            nc.scalar.activation(
+                out=dropped[:],
+                in_=x_t_block[:],
+                func=ACT.Square,
+                bias=neg_mean[:, j : j + 1],
+                accum_out=sum_sq[:, j : j + 1],
+            )
+            return x_t_block
 
+        def slopes_and_shifts(g):
+            blocks = slice(g * PACK, (g + 1) * PACK)
+            beta_blocks = slice(FEATURE_BLOCKS + g * PACK, FEATURE_BLOCKS + (g + 1) * PACK)
             nc.scalar.activation(
                 out=std[:, blocks], in_=sum_sq[:, blocks], func=ACT.Sqrt,
                 bias=eps[:, 0:1], scale=1.0 / BATCH,
             )
             nc.vector.reciprocal(out=rstd[:, blocks], in_=std[:, blocks])
-            nc.vector.tensor_mul(out=slope[:, blocks], in0=gamma_cols[:, blocks], in1=rstd[:, blocks])
+            nc.vector.tensor_mul(out=slope[:, blocks], in0=gb_cols[:, blocks], in1=rstd[:, blocks])
             nc.vector.tensor_mul(
                 out=neg_mean_slope[:, blocks], in0=neg_mean[:, blocks], in1=slope[:, blocks]
             )
             nc.vector.tensor_add(
-                out=shift[:, blocks], in0=neg_mean_slope[:, blocks], in1=beta_cols[:, blocks]
+                out=shift[:, blocks], in0=neg_mean_slope[:, blocks], in1=gb_cols[:, beta_blocks]
             )
 
-            normed = h_stage.tile([P, PACK, BATCH], BF16)
+        def norm(g, x_t):
+            normed = normed_pool.tile([P, PACK, BATCH], BF16)
             for t in range(PACK):
                 j = g * PACK + t
-                nc.vector.tensor_scalar(
-                    out=normed[:, t, :],
-                    in0=x_t[t][:],
-                    scalar1=slope[:, j : j + 1],
-                    scalar2=shift[:, j : j + 1],
-                    op0=ALU.mult,
-                    op1=ALU.add,
-                )
-            grouped = h_stage.tile([P, BATCH, PACK], BF16, align_bytes=64)
-            nc.vector.tensor_scalar_max(
-                out=grouped[:].rearrange("p (c i) t -> p c t i", i=4),
-                in0=normed[:].rearrange("p t (c i) -> p c t i", i=4),
-                scalar1=0.0,
-            )
-            codes = keep.tile([P, BATCH], U32, name="h_codes%d" % g, align_bytes=64)
-            scales = keep.tile([P, BATCH], U8, name="h_scales%d" % g, align_bytes=64)
-            nc.vector.quantize_mx(
-                out=codes[:].bitcast(FP8X4),
-                scales=scales[:],
-                in_=grouped[:].rearrange("p r t -> p (r t)"),
-            )
-            h_codes.append(codes)
-            h_scales.append(scales)
+                if t == SCALAR_NORM_BLOCK:
+                    nc.scalar.activation(
+                        out=normed[:, t, :], in_=x_t[t][:], func=ACT.Identity,
+                        bias=shift[:, j : j + 1], scale=slope[:, j : j + 1],
+                    )
+                else:
+                    nc.vector.tensor_scalar(
+                        out=normed[:, t, :], in0=x_t[t][:],
+                        scalar1=slope[:, j : j + 1], scalar2=shift[:, j : j + 1],
+                        op0=ALU.mult, op1=ALU.add,
+                    )
+            return normed
 
-        def quantise_w_chunk(c):
-            chunk_codes = []
-            chunk_scales = []
-            for g in range(PASSES):
-                grouped = w_stage.tile([P, N_TILE, PACK], BF16, align_bytes=64, name="w_grouped")
-                nc.scalar.copy(
+        h_codes = [[None] * HALVES for g in range(PASSES)]
+        h_scales = [[None] * HALVES for g in range(PASSES)]
+
+        def relu_and_quantise(g, normed):
+            h_grouped = []
+            for half in range(HALVES):
+                rows = slice(half * HALF_BATCH, (half + 1) * HALF_BATCH)
+                grouped = grouped_pool.tile([P, HALF_BATCH, PACK], BF16, align_bytes=64, tag="grouped")
+                nc.vector.tensor_scalar_max(
                     out=grouped[:].rearrange("p (c i) t -> p c t i", i=4),
-                    in_=w_raw[c][:, g * PACK : (g + 1) * PACK, :].rearrange(
-                        "p t (c i) -> p c t i", i=4
-                    ),
+                    in0=normed[:, :, rows].rearrange("p t (c i) -> p c t i", i=4),
+                    scalar1=0.0,
                 )
-                codes = keep.tile([P, N_TILE], U32, name="w_codes%d_%d" % (c, g), align_bytes=64)
-                scales = keep.tile([P, N_TILE], U8, name="w_scales%d_%d" % (c, g), align_bytes=64)
+                h_grouped.append(grouped)
+            for half in range(HALVES):
+                codes = keep.tile([P, HALF_BATCH], U32, name="h_codes%d_%d" % (g, half), align_bytes=64)
+                scales = keep.tile([P, HALF_BATCH], U8, name="h_scales%d_%d" % (g, half), align_bytes=64)
                 nc.vector.quantize_mx(
                     out=codes[:].bitcast(FP8X4),
                     scales=scales[:],
-                    in_=grouped[:].rearrange("p n t -> p (n t)"),
+                    in_=h_grouped[half][:].rearrange("p r t -> p (r t)"),
                 )
-                chunk_codes.append(codes)
-                chunk_scales.append(scales)
-            return chunk_codes, chunk_scales
+                h_codes[g][half] = codes
+                h_scales[g][half] = scales
 
-        w_next = quantise_w_chunk(0)
+        w_codes = [[None] * PASSES for c in range(OUT_CHUNKS)]
+        w_scales = [[None] * PASSES for c in range(OUT_CHUNKS)]
+
+        def regroup_w(copy_engine_op, c, g):
+            slots = slice((g % HALF_PASSES) * PACK, (g % HALF_PASSES + 1) * PACK)
+            grouped = grouped_pool.tile([P, N_TILE, PACK], BF16, align_bytes=64, tag="grouped")
+            copy_engine_op(
+                out=grouped[:].rearrange("p (c i) t -> p c t i", i=4),
+                in_=w_raw[c][g // HALF_PASSES][:, slots, :].rearrange("p t (c i) -> p c t i", i=4),
+            )
+            return grouped
+
+        def quantise_w(c, g, grouped):
+            codes = keep.tile([P, N_TILE], U32, name="w_codes%d_%d" % (c, g), align_bytes=64)
+            scales = keep.tile([P, N_TILE], U8, name="w_scales%d_%d" % (c, g), align_bytes=64)
+            nc.vector.quantize_mx(
+                out=codes[:].bitcast(FP8X4),
+                scales=scales[:],
+                in_=grouped[:].rearrange("p n t -> p (n t)"),
+            )
+            w_codes[c][g] = codes
+            w_scales[c][g] = scales
+
+        x_t_of = [None] * PASSES
+        for g in range(PASSES + 1):
+            if g > 0:
+                slopes_and_shifts(g - 1)
+            if g < PASSES:
+                means(g)
+                x_t_of[g] = [transpose_and_square(g, 0)]
+            if g > 0:
+                normed = norm(g - 1, x_t_of[g - 1])
+            if g < PASSES:
+                for t in range(1, PACK):
+                    x_t_of[g].append(transpose_and_square(g, t))
+            if g == 0:
+                first_units = [regroup_w(nc.vector.tensor_copy, 0, u) for u in range(HALF_PASSES)]
+                for u in range(HALF_PASSES):
+                    quantise_w(0, u, first_units[u])
+            if g > 0:
+                relu_and_quantise(g - 1, normed)
+        for g in range(HALF_PASSES, PASSES):
+            quantise_w(0, g, regroup_w(nc.scalar.copy, 0, g))
+
         for c in range(OUT_CHUNKS):
-            w_codes, w_scales = w_next
-            if c + 1 < OUT_CHUNKS:
-                w_next = quantise_w_chunk(c + 1)
             n_cols = slice(c * N_TILE, (c + 1) * N_TILE)
             for m in range(ROW_BLOCKS):
-                m_cols = slice(m * P, (m + 1) * P)
+                half = m // (ROW_BLOCKS // HALVES)
+                m_cols = slice((m % (ROW_BLOCKS // HALVES)) * P, (m % (ROW_BLOCKS // HALVES) + 1) * P)
                 acc = banks.tile([P, N_TILE], F32, tag="bank")
                 for g in range(PASSES):
                     nc.tensor.matmul_mx(
                         out=acc[:],
-                        lhsT=h_codes[g][:, m_cols].bitcast(FP8X4),
-                        lhsT_scale=h_scales[g][:, m_cols],
-                        rhs=w_codes[g][:].bitcast(FP8X4),
-                        rhs_scale=w_scales[g][:],
+                        lhsT=h_codes[g][half][:, m_cols].bitcast(FP8X4),
+                        lhsT_scale=h_scales[g][half][:, m_cols],
+                        rhs=w_codes[c][g][:].bitcast(FP8X4),
+                        rhs_scale=w_scales[c][g][:],
                         start=(g == 0),
                         stop=(g == PASSES - 1),
                     )
@@ -213,4 +266,6 @@ def tile_customnetwork_pa_kernel(tc, h_lin, gamma, beta, w, b, out):
                 nc.vector.tensor_tensor(
                     out=result[:], in0=acc[:], in1=bias_all[:, n_cols], op=ALU.add
                 )
-                nc.sync.dma_start(out=out[m_cols, n_cols], in_=result[:])
+                nc.sync.dma_start(out=out[m * P : (m + 1) * P, n_cols], in_=result[:])
+                if c + 1 < OUT_CHUNKS and m % 2 == 1:
+                    quantise_w(c + 1, m // 2, regroup_w(nc.scalar.copy, c + 1, m // 2))

@@ -15,7 +15,7 @@ P = 128
 PACK = 4
 K_PASS = P * PACK
 N_TILE = 512
-MEAN_COLS = 32
+MEAN_COLS = 128
 BN_EPS = 1e-5
 
 BATCH, D_IN, D_OUT = 1024, 2048, 2048
@@ -28,7 +28,6 @@ OUT_CHUNKS = D_OUT // N_TILE
 HALVES = 2
 HALF_BATCH = BATCH // HALVES
 HALF_PASSES = PASSES // HALVES
-SCALAR_NORM_BLOCK = PACK - 1
 
 
 def tile_customnetwork_pa_kernel(tc, h_lin, gamma, beta, w, b, out):
@@ -39,10 +38,9 @@ def tile_customnetwork_pa_kernel(tc, h_lin, gamma, beta, w, b, out):
         keep = ctx.enter_context(tc.tile_pool(name="keep", bufs=1))
         normed_pool = ctx.enter_context(tc.tile_pool(name="normed_pool", bufs=2))
         squares = ctx.enter_context(tc.tile_pool(name="squares", bufs=4))
-        grouped_pool = ctx.enter_context(tc.tile_pool(name="grouped_pool", bufs=4))
+        grouped_pool = ctx.enter_context(tc.tile_pool(name="grouped_pool", bufs=6))
         out_stage = ctx.enter_context(tc.tile_pool(name="out_stage", bufs=6))
-        mean_bank = ctx.enter_context(tc.psum_pool(name="mean_bank", bufs=1))
-        banks = ctx.enter_context(tc.psum_pool(name="banks", bufs=7))
+        banks = ctx.enter_context(tc.psum_pool(name="banks", bufs=8))
 
         x_sb = [
             keep.tile([P, ROW_BLOCKS, K_PASS], BF16, name="x%d" % g) for g in range(PASSES)
@@ -103,27 +101,31 @@ def tile_customnetwork_pa_kernel(tc, h_lin, gamma, beta, w, b, out):
         gb_cols = const.tile([P, 2 * FEATURE_BLOCKS], F32)
         nc.vector.tensor_copy(out=gb_cols[:], in_=gb_ps[:, 0 : 2 * FEATURE_BLOCKS])
 
-        neg_mean_ps = mean_bank.tile([P, FEATURE_BLOCKS, MEAN_COLS], F32)
         neg_mean = const.tile([P, FEATURE_BLOCKS], F32)
         sum_sq = const.tile([P, FEATURE_BLOCKS], F32)
         std = const.tile([P, FEATURE_BLOCKS], F32)
         rstd = const.tile([P, FEATURE_BLOCKS], F32)
         slope = const.tile([P, FEATURE_BLOCKS], F32)
+        neg_mean_gamma = const.tile([P, FEATURE_BLOCKS], F32)
         neg_mean_slope = const.tile([P, FEATURE_BLOCKS], F32)
         shift = const.tile([P, FEATURE_BLOCKS], F32)
 
         def means(g):
+            neg_mean_ps = banks.tile([P, PACK, MEAN_COLS], F32, tag="bank")
             for t in range(PACK):
                 for r in range(ROW_BLOCKS):
                     nc.tensor.matmul(
-                        out=neg_mean_ps[:, g * PACK + t, :],
+                        out=neg_mean_ps[:, t, :],
                         lhsT=x_sb[g][:, r, t * P : (t + 1) * P],
                         rhs=minus_inv_batch[:],
                         start=(r == 0),
                         stop=(r == ROW_BLOCKS - 1),
                     )
             blocks = slice(g * PACK, (g + 1) * PACK)
-            nc.scalar.copy(out=neg_mean[:, blocks], in_=neg_mean_ps[:, blocks, 0])
+            nc.scalar.copy(out=neg_mean[:, blocks], in_=neg_mean_ps[:, :, 0])
+            nc.vector.tensor_mul(
+                out=neg_mean_gamma[:, blocks], in0=neg_mean[:, blocks], in1=gb_cols[:, blocks]
+            )
 
         def transpose_and_square(g, t):
             j = g * PACK + t
@@ -152,10 +154,10 @@ def tile_customnetwork_pa_kernel(tc, h_lin, gamma, beta, w, b, out):
                 bias=eps[:, 0:1], scale=1.0 / BATCH,
             )
             nc.vector.reciprocal(out=rstd[:, blocks], in_=std[:, blocks])
-            nc.vector.tensor_mul(out=slope[:, blocks], in0=gb_cols[:, blocks], in1=rstd[:, blocks])
             nc.vector.tensor_mul(
-                out=neg_mean_slope[:, blocks], in0=neg_mean[:, blocks], in1=slope[:, blocks]
+                out=neg_mean_slope[:, blocks], in0=neg_mean_gamma[:, blocks], in1=rstd[:, blocks]
             )
+            nc.vector.tensor_mul(out=slope[:, blocks], in0=gb_cols[:, blocks], in1=rstd[:, blocks])
             nc.vector.tensor_add(
                 out=shift[:, blocks], in0=neg_mean_slope[:, blocks], in1=gb_cols[:, beta_blocks]
             )
@@ -164,17 +166,11 @@ def tile_customnetwork_pa_kernel(tc, h_lin, gamma, beta, w, b, out):
             normed = normed_pool.tile([P, PACK, BATCH], BF16)
             for t in range(PACK):
                 j = g * PACK + t
-                if t == SCALAR_NORM_BLOCK:
-                    nc.scalar.activation(
-                        out=normed[:, t, :], in_=x_t[t][:], func=ACT.Identity,
-                        bias=shift[:, j : j + 1], scale=slope[:, j : j + 1],
-                    )
-                else:
-                    nc.vector.tensor_scalar(
-                        out=normed[:, t, :], in0=x_t[t][:],
-                        scalar1=slope[:, j : j + 1], scalar2=shift[:, j : j + 1],
-                        op0=ALU.mult, op1=ALU.add,
-                    )
+                nc.vector.tensor_scalar(
+                    out=normed[:, t, :], in0=x_t[t][:],
+                    scalar1=slope[:, j : j + 1], scalar2=shift[:, j : j + 1],
+                    op0=ALU.mult, op1=ALU.add,
+                )
             return normed
 
         h_codes = [[None] * HALVES for g in range(PASSES)]
@@ -225,47 +221,67 @@ def tile_customnetwork_pa_kernel(tc, h_lin, gamma, beta, w, b, out):
             w_codes[c][g] = codes
             w_scales[c][g] = scales
 
-        x_t_of = [None] * PASSES
-        for g in range(PASSES + 1):
-            if g > 0:
-                slopes_and_shifts(g - 1)
-            if g < PASSES:
-                means(g)
-                x_t_of[g] = [transpose_and_square(g, 0)]
-            if g > 0:
-                normed = norm(g - 1, x_t_of[g - 1])
-            if g < PASSES:
-                for t in range(1, PACK):
-                    x_t_of[g].append(transpose_and_square(g, t))
-            if g == 0:
-                first_units = [regroup_w(nc.vector.tensor_copy, 0, u) for u in range(HALF_PASSES)]
-                for u in range(HALF_PASSES):
-                    quantise_w(0, u, first_units[u])
-            if g > 0:
-                relu_and_quantise(g - 1, normed)
-        for g in range(HALF_PASSES, PASSES):
-            quantise_w(0, g, regroup_w(nc.scalar.copy, 0, g))
+        TILES_PER_HALF = ROW_BLOCKS // HALVES
+
+        def mx_passes(acc, c, m, passes):
+            half = m // TILES_PER_HALF
+            m_cols = slice((m % TILES_PER_HALF) * P, (m % TILES_PER_HALF + 1) * P)
+            for g in passes:
+                nc.tensor.matmul_mx(
+                    out=acc[:],
+                    lhsT=h_codes[g][half][:, m_cols].bitcast(FP8X4),
+                    lhsT_scale=h_scales[g][half][:, m_cols],
+                    rhs=w_codes[c][g][:].bitcast(FP8X4),
+                    rhs_scale=w_scales[c][g][:],
+                    start=(g == 0),
+                    stop=(g == PASSES - 1),
+                )
+
+        means(0)
+        x_t = [transpose_and_square(0, t) for t in range(PACK)]
+        first_units = [regroup_w(nc.vector.tensor_copy, 0, g) for g in range(HALF_PASSES)]
+        for g in range(HALF_PASSES):
+            quantise_w(0, g, first_units[g])
+        for g in range(1, PASSES):
+            means(g)
+            slopes_and_shifts(g - 1)
+            x_t_next = [transpose_and_square(g, 0)]
+            normed = norm(g - 1, x_t)
+            for t in range(1, PACK):
+                x_t_next.append(transpose_and_square(g, t))
+            relu_and_quantise(g - 1, normed)
+            x_t = x_t_next
+        last = PASSES - 1
+        slopes_and_shifts(last)
+        late_units = [regroup_w(nc.scalar.copy, 0, g) for g in range(HALF_PASSES, PASSES)]
+        normed = norm(last, x_t)
+        quantise_w(0, HALF_PASSES, late_units[0])
+        first_accs = []
+        for half in range(HALVES):
+            tiles = range(half * TILES_PER_HALF, (half + 1) * TILES_PER_HALF)
+            for m in tiles:
+                first_accs.append(banks.tile([P, N_TILE], F32, tag="bank", name="acc"))
+            for g in range(last):
+                for m in tiles:
+                    mx_passes(first_accs[m], 0, m, [g])
+        relu_and_quantise(last, normed)
+        quantise_w(0, last, late_units[1])
 
         for c in range(OUT_CHUNKS):
             n_cols = slice(c * N_TILE, (c + 1) * N_TILE)
+            if c + 1 < OUT_CHUNKS:
+                next_units = [regroup_w(nc.scalar.copy, c + 1, g) for g in range(PASSES)]
             for m in range(ROW_BLOCKS):
-                half = m // (ROW_BLOCKS // HALVES)
-                m_cols = slice((m % (ROW_BLOCKS // HALVES)) * P, (m % (ROW_BLOCKS // HALVES) + 1) * P)
-                acc = banks.tile([P, N_TILE], F32, tag="bank")
-                for g in range(PASSES):
-                    nc.tensor.matmul_mx(
-                        out=acc[:],
-                        lhsT=h_codes[g][half][:, m_cols].bitcast(FP8X4),
-                        lhsT_scale=h_scales[g][half][:, m_cols],
-                        rhs=w_codes[c][g][:].bitcast(FP8X4),
-                        rhs_scale=w_scales[c][g][:],
-                        start=(g == 0),
-                        stop=(g == PASSES - 1),
-                    )
+                if c == 0:
+                    acc = first_accs[m]
+                    mx_passes(acc, c, m, [last])
+                else:
+                    acc = banks.tile([P, N_TILE], F32, tag="bank", name="acc")
+                    mx_passes(acc, c, m, range(PASSES))
                 result = out_stage.tile([P, N_TILE], F32)
                 nc.vector.tensor_tensor(
                     out=result[:], in0=acc[:], in1=bias_all[:, n_cols], op=ALU.add
                 )
                 nc.sync.dma_start(out=out[m * P : (m + 1) * P, n_cols], in_=result[:])
-                if c + 1 < OUT_CHUNKS and m % 2 == 1:
-                    quantise_w(c + 1, m // 2, regroup_w(nc.scalar.copy, c + 1, m // 2))
+                if c + 1 < OUT_CHUNKS and m % 2 == 0:
+                    quantise_w(c + 1, m // 2, next_units[m // 2])

@@ -28,6 +28,7 @@ OUT_CHUNKS = D_OUT // N_TILE
 HALVES = 2
 HALF_BATCH = BATCH // HALVES
 HALF_PASSES = PASSES // HALVES
+RUNS_PER_LOAD = 4
 
 
 def tile_customnetwork_pa_kernel(tc, h_lin, gamma, beta, w, b, out):
@@ -46,25 +47,25 @@ def tile_customnetwork_pa_kernel(tc, h_lin, gamma, beta, w, b, out):
             keep.tile([P, ROW_BLOCKS, K_PASS], BF16, name="x%d" % g) for g in range(PASSES)
         ]
         w_raw = [
-            [
-                keep.tile([P, HALF_PASSES * PACK, N_TILE], BF16, name="w_raw%d_%d" % (c, half))
-                for half in range(HALVES)
-            ]
+            [keep.tile([P, PACK, N_TILE], BF16, name="w_raw%d_%d" % (c, g)) for g in range(PASSES)]
             for c in range(OUT_CHUNKS)
         ]
         bias_all = const.tile([P, D_OUT], BF16)
 
         def load_x(g):
-            nc.sync.dma_start(
-                out=x_sb[g][:],
-                in_=h_lin[:, g * K_PASS : (g + 1) * K_PASS].rearrange("(r p) d -> p r d", p=P),
-            )
+            columns = h_lin[:, g * K_PASS : (g + 1) * K_PASS].rearrange("(r p) d -> p r d", p=P)
+            for r in range(0, ROW_BLOCKS, RUNS_PER_LOAD):
+                nc.sync.dma_start(
+                    out=x_sb[g][:, r : r + RUNS_PER_LOAD, :],
+                    in_=columns[:, r : r + RUNS_PER_LOAD, :],
+                )
 
-        def load_w(c, half):
-            rows = slice(half * HALF_PASSES * K_PASS, (half + 1) * HALF_PASSES * K_PASS)
+        def load_w(c, g):
             nc.sync.dma_start(
-                out=w_raw[c][half][:],
-                in_=w[rows, c * N_TILE : (c + 1) * N_TILE].rearrange("(j p) n -> p j n", p=P),
+                out=w_raw[c][g][:],
+                in_=w[g * K_PASS : (g + 1) * K_PASS, c * N_TILE : (c + 1) * N_TILE].rearrange(
+                    "(t p) n -> p t n", p=P
+                ),
             )
 
         gb_rows = const.tile([P, P], BF16)
@@ -79,14 +80,16 @@ def tile_customnetwork_pa_kernel(tc, h_lin, gamma, beta, w, b, out):
         nc.vector.memset(gb_rows[64:128, :], 0.0)
         load_x(0)
         load_w(0, 0)
-        load_x(1)
         load_w(0, 1)
+        load_x(1)
+        load_w(0, 2)
+        load_w(0, 3)
         load_x(2)
         load_x(3)
         nc.sync.dma_start(out=bias_all[:], in_=b.partition_broadcast(P))
         for c in range(1, OUT_CHUNKS):
-            for half in range(HALVES):
-                load_w(c, half)
+            for g in range(PASSES):
+                load_w(c, g)
 
         ident = const.tile([P, P], BF16)
         masks.make_identity(nc, ident[:])
@@ -202,11 +205,10 @@ def tile_customnetwork_pa_kernel(tc, h_lin, gamma, beta, w, b, out):
         w_scales = [[None] * PASSES for c in range(OUT_CHUNKS)]
 
         def regroup_w(copy_engine_op, c, g):
-            slots = slice((g % HALF_PASSES) * PACK, (g % HALF_PASSES + 1) * PACK)
             grouped = grouped_pool.tile([P, N_TILE, PACK], BF16, align_bytes=64, tag="grouped")
             copy_engine_op(
                 out=grouped[:].rearrange("p (c i) t -> p c t i", i=4),
-                in_=w_raw[c][g // HALF_PASSES][:, slots, :].rearrange("p t (c i) -> p c t i", i=4),
+                in_=w_raw[c][g][:].rearrange("p t (c i) -> p c t i", i=4),
             )
             return grouped
 

@@ -31,21 +31,25 @@ HALF_PASSES = PASSES // HALVES
 RUNS_PER_LOAD = 4
 
 
+W_BUFS = 3
+
+
 def tile_customnetwork_pa_kernel(tc, h_lin, gamma, beta, w, b, out):
     nc = tc.nc
     with ExitStack() as ctx:
         ctx.enter_context(tc.manual_schedule())
         const = ctx.enter_context(tc.tile_pool(name="const", bufs=1))
         keep = ctx.enter_context(tc.tile_pool(name="keep", bufs=1))
-        normed_pool = ctx.enter_context(tc.tile_pool(name="normed_pool", bufs=2))
-        squares = ctx.enter_context(tc.tile_pool(name="squares", bufs=4))
-        grouped_pool = ctx.enter_context(tc.tile_pool(name="grouped_pool", bufs=6))
+        wide = ctx.enter_context(tc.tile_pool(name="wide", bufs=6))
+        squares = ctx.enter_context(tc.tile_pool(name="squares", bufs=1))
+        h_pool = ctx.enter_context(tc.tile_pool(name="h_pool", bufs=2))
+        h1_pool = ctx.enter_context(tc.tile_pool(name="h1_pool", bufs=4))
+        w_pool = ctx.enter_context(tc.tile_pool(name="w_pool", bufs=W_BUFS))
+        ring = ctx.enter_context(tc.tile_pool(name="ring", bufs=1))
         out_stage = ctx.enter_context(tc.tile_pool(name="out_stage", bufs=6))
         banks = ctx.enter_context(tc.psum_pool(name="banks", bufs=8))
 
-        x_sb = [
-            keep.tile([P, ROW_BLOCKS, K_PASS], BF16, name="x%d" % g) for g in range(PASSES)
-        ]
+        x_sb = [wide.tile([P, ROW_BLOCKS, K_PASS], BF16, tag="wide", name="x%d" % g) for g in range(PASSES)]
         w_raw = [
             [keep.tile([P, PACK, N_TILE], BF16, name="w_raw%d_%d" % (c, g)) for g in range(PASSES)]
             for c in range(OUT_CHUNKS)
@@ -112,6 +116,7 @@ def tile_customnetwork_pa_kernel(tc, h_lin, gamma, beta, w, b, out):
         neg_mean_gamma = const.tile([P, FEATURE_BLOCKS], F32)
         neg_mean_slope = const.tile([P, FEATURE_BLOCKS], F32)
         shift = const.tile([P, FEATURE_BLOCKS], F32)
+        small = nc.vector
 
         def means(g):
             neg_mean_ps = banks.tile([P, PACK, MEAN_COLS], F32, tag="bank")
@@ -126,7 +131,10 @@ def tile_customnetwork_pa_kernel(tc, h_lin, gamma, beta, w, b, out):
                     )
             blocks = slice(g * PACK, (g + 1) * PACK)
             nc.scalar.copy(out=neg_mean[:, blocks], in_=neg_mean_ps[:, :, 0])
-            nc.vector.tensor_mul(
+
+        def mean_times_gamma(g):
+            blocks = slice(g * PACK, (g + 1) * PACK)
+            small.tensor_mul(
                 out=neg_mean_gamma[:, blocks], in0=neg_mean[:, blocks], in1=gb_cols[:, blocks]
             )
 
@@ -157,16 +165,16 @@ def tile_customnetwork_pa_kernel(tc, h_lin, gamma, beta, w, b, out):
                 bias=eps[:, 0:1], scale=1.0 / BATCH,
             )
             nc.vector.reciprocal(out=rstd[:, blocks], in_=std[:, blocks])
-            nc.vector.tensor_mul(
+            small.tensor_mul(
                 out=neg_mean_slope[:, blocks], in0=neg_mean_gamma[:, blocks], in1=rstd[:, blocks]
             )
-            nc.vector.tensor_mul(out=slope[:, blocks], in0=gb_cols[:, blocks], in1=rstd[:, blocks])
-            nc.vector.tensor_add(
+            small.tensor_mul(out=slope[:, blocks], in0=gb_cols[:, blocks], in1=rstd[:, blocks])
+            small.tensor_add(
                 out=shift[:, blocks], in0=neg_mean_slope[:, blocks], in1=gb_cols[:, beta_blocks]
             )
 
         def norm(g, x_t):
-            normed = normed_pool.tile([P, PACK, BATCH], BF16)
+            normed = wide.tile([P, PACK, BATCH], BF16, tag="wide", name="normed%d" % g)
             for t in range(PACK):
                 j = g * PACK + t
                 nc.vector.tensor_scalar(
@@ -179,111 +187,192 @@ def tile_customnetwork_pa_kernel(tc, h_lin, gamma, beta, w, b, out):
         h_codes = [[None] * HALVES for g in range(PASSES)]
         h_scales = [[None] * HALVES for g in range(PASSES)]
 
-        def relu_and_quantise(g, normed):
-            h_grouped = []
-            for half in range(HALVES):
-                rows = slice(half * HALF_BATCH, (half + 1) * HALF_BATCH)
-                grouped = grouped_pool.tile([P, HALF_BATCH, PACK], BF16, align_bytes=64, tag="grouped")
-                nc.vector.tensor_scalar_max(
-                    out=grouped[:].rearrange("p (c i) t -> p c t i", i=4),
-                    in0=normed[:, :, rows].rearrange("p t (c i) -> p c t i", i=4),
-                    scalar1=0.0,
-                )
-                h_grouped.append(grouped)
-            for half in range(HALVES):
-                codes = keep.tile([P, HALF_BATCH], U32, name="h_codes%d_%d" % (g, half), align_bytes=64)
-                scales = keep.tile([P, HALF_BATCH], U8, name="h_scales%d_%d" % (g, half), align_bytes=64)
-                nc.vector.quantize_mx(
-                    out=codes[:].bitcast(FP8X4),
-                    scales=scales[:],
-                    in_=h_grouped[half][:].rearrange("p r t -> p (r t)"),
-                )
-                h_codes[g][half] = codes
-                h_scales[g][half] = scales
+        def relu_regroup(on_scalar, normed, half):
+            rows = slice(half * HALF_BATCH, (half + 1) * HALF_BATCH)
+            pool = h1_pool if half else h_pool
+            grouped = pool.tile([P, HALF_BATCH, PACK], BF16, align_bytes=64, tag="h_grouped")
+            dst = grouped[:].rearrange("p (c i) t -> p c t i", i=4)
+            src = normed[:, :, rows].rearrange("p t (c i) -> p c t i", i=4)
+            if on_scalar:
+                nc.scalar.activation(out=dst, in_=src, func=ACT.Relu)
+            else:
+                nc.vector.tensor_scalar_max(out=dst, in0=src, scalar1=0.0)
+            return grouped
+
+        def quantise_h(g, half, grouped):
+            codes = keep.tile([P, HALF_BATCH], U32, name="h_codes%d_%d" % (g, half), align_bytes=64)
+            scales = keep.tile([P, HALF_BATCH], U8, name="h_scales%d_%d" % (g, half), align_bytes=64)
+            nc.vector.quantize_mx(
+                out=codes[:].bitcast(FP8X4),
+                scales=scales[:],
+                in_=grouped[:].rearrange("p r t -> p (r t)"),
+            )
+            h_codes[g][half] = codes
+            h_scales[g][half] = scales
 
         w_codes = [[None] * PASSES for c in range(OUT_CHUNKS)]
         w_scales = [[None] * PASSES for c in range(OUT_CHUNKS)]
+        w_grouped = {}
 
         def regroup_w(copy_engine_op, c, g):
-            grouped = grouped_pool.tile([P, N_TILE, PACK], BF16, align_bytes=64, tag="grouped")
+            grouped = w_pool.tile([P, N_TILE, PACK], BF16, align_bytes=64, tag="w_grouped")
             copy_engine_op(
                 out=grouped[:].rearrange("p (c i) t -> p c t i", i=4),
                 in_=w_raw[c][g][:].rearrange("p t (c i) -> p c t i", i=4),
             )
-            return grouped
+            w_grouped[(c, g)] = grouped
 
-        def quantise_w(c, g, grouped):
+        def regroup_w_ring(on_gpsimd, c, g):
+            grouped = ring.tile([P, N_TILE, PACK], BF16, align_bytes=64, tag="ring")
+            dst = grouped[:].rearrange("p (c i) t -> p c t i", i=4)
+            src = w_raw[c][g][:].rearrange("p t (c i) -> p c t i", i=4)
+            if on_gpsimd:
+                nc.gpsimd.tensor_scalar(
+                    out=dst, in0=src, scalar1=1.0, scalar2=0.0, op0=ALU.mult, op1=ALU.add
+                )
+            else:
+                nc.vector.tensor_copy(out=dst, in_=src)
+            w_grouped[(c, g)] = grouped
+
+        def quantise_w(c, g):
             codes = keep.tile([P, N_TILE], U32, name="w_codes%d_%d" % (c, g), align_bytes=64)
             scales = keep.tile([P, N_TILE], U8, name="w_scales%d_%d" % (c, g), align_bytes=64)
             nc.vector.quantize_mx(
                 out=codes[:].bitcast(FP8X4),
                 scales=scales[:],
-                in_=grouped[:].rearrange("p n t -> p (n t)"),
+                in_=w_grouped[(c, g)][:].rearrange("p n t -> p (n t)"),
             )
             w_codes[c][g] = codes
             w_scales[c][g] = scales
 
         TILES_PER_HALF = ROW_BLOCKS // HALVES
+        accs = {}
 
-        def mx_passes(acc, c, m, passes):
+        def open_tiles(c, half):
+            for m in range(half * TILES_PER_HALF, (half + 1) * TILES_PER_HALF):
+                accs[(c, m)] = banks.tile([P, N_TILE], F32, tag="bank", name="acc")
+
+        def mx_pass(c, m, g):
             half = m // TILES_PER_HALF
             m_cols = slice((m % TILES_PER_HALF) * P, (m % TILES_PER_HALF + 1) * P)
-            for g in passes:
-                nc.tensor.matmul_mx(
-                    out=acc[:],
-                    lhsT=h_codes[g][half][:, m_cols].bitcast(FP8X4),
-                    lhsT_scale=h_scales[g][half][:, m_cols],
-                    rhs=w_codes[c][g][:].bitcast(FP8X4),
-                    rhs_scale=w_scales[c][g][:],
-                    start=(g == 0),
-                    stop=(g == PASSES - 1),
-                )
+            nc.tensor.matmul_mx(
+                out=accs[(c, m)][:],
+                lhsT=h_codes[g][half][:, m_cols].bitcast(FP8X4),
+                lhsT_scale=h_scales[g][half][:, m_cols],
+                rhs=w_codes[c][g][:].bitcast(FP8X4),
+                rhs_scale=w_scales[c][g][:],
+                start=(g == 0),
+                stop=(g == PASSES - 1),
+            )
 
+        def mx_half(c, half, g):
+            for m in range(half * TILES_PER_HALF, (half + 1) * TILES_PER_HALF):
+                mx_pass(c, m, g)
+
+        def finish(c, m):
+            n_cols = slice(c * N_TILE, (c + 1) * N_TILE)
+            result = out_stage.tile([P, N_TILE], F32, name="result")
+            nc.vector.tensor_tensor(
+                out=result[:], in0=accs[(c, m)][:], in1=bias_all[:, n_cols], op=ALU.add
+            )
+            nc.sync.dma_start(out=out[m * P : (m + 1) * P, n_cols], in_=result[:])
+
+        last = PASSES - 1
         means(0)
         x_t = [transpose_and_square(0, t) for t in range(PACK)]
-        first_units = [regroup_w(nc.vector.tensor_copy, 0, g) for g in range(HALF_PASSES)]
-        for g in range(HALF_PASSES):
-            quantise_w(0, g, first_units[g])
-        for g in range(1, PASSES):
-            means(g)
-            slopes_and_shifts(g - 1)
-            x_t_next = [transpose_and_square(g, 0)]
-            normed = norm(g - 1, x_t)
-            for t in range(1, PACK):
-                x_t_next.append(transpose_and_square(g, t))
-            relu_and_quantise(g - 1, normed)
+        for g in (0, 1):
+            regroup_w(nc.vector.tensor_copy, 0, g)
+        for g in (0, 1):
+            quantise_w(0, g)
+        regroup_w(nc.vector.tensor_copy, 0, 2)
+        regroup_w_ring(False, 0, 3)
+        quantise_w(0, 2)
+        mean_times_gamma(0)
+        in_ring = [(0, 3), (1, 0), (1, 1), (1, 2)]
+        normed = [None] * PASSES
+        for g in range(PASSES):
+            if g < last:
+                means(g + 1)
+            slopes_and_shifts(g)
+            if g > 0:
+                quantise_w(*in_ring[g - 1])
+                regroup_w_ring(True, *in_ring[g])
+            x_t_next = []
+            if g < last:
+                x_t_next.append(transpose_and_square(g + 1, 0))
+            normed[g] = norm(g, x_t)
+            if g < last:
+                for t in range(1, PACK):
+                    x_t_next.append(transpose_and_square(g + 1, t))
+            grouped = relu_regroup(False, normed[g], 0)
+            if g < last:
+                mean_times_gamma(g + 1)
+            quantise_h(g, 0, grouped)
             x_t = x_t_next
-        last = PASSES - 1
-        slopes_and_shifts(last)
-        late_units = [regroup_w(nc.scalar.copy, 0, g) for g in range(HALF_PASSES, PASSES)]
-        normed = norm(last, x_t)
-        quantise_w(0, HALF_PASSES, late_units[0])
-        first_accs = []
-        for half in range(HALVES):
-            tiles = range(half * TILES_PER_HALF, (half + 1) * TILES_PER_HALF)
-            for m in tiles:
-                first_accs.append(banks.tile([P, N_TILE], F32, tag="bank", name="acc"))
-            for g in range(last):
-                for m in tiles:
-                    mx_passes(first_accs[m], 0, m, [g])
-        relu_and_quantise(last, normed)
-        quantise_w(0, last, late_units[1])
+            if g == last - 1:
+                open_tiles(0, 0)
+                for gg in range(last):
+                    mx_half(0, 0, gg)
+        open_tiles(1, 0)
+        mx_half(1, 0, 0)
+        mx_half(1, 0, 1)
+        regroup_w(nc.scalar.copy, 1, 3)
+        h1 = {}
+        for g in range(PASSES):
+            h1[g] = relu_regroup(True, normed[g], 1)
+        scalar_units = [(c, g) for c in (2, 3) for g in range(PASSES)]
+        counts = [0, 1]
 
-        for c in range(OUT_CHUNKS):
-            n_cols = slice(c * N_TILE, (c + 1) * N_TILE)
-            if c + 1 < OUT_CHUNKS:
-                next_units = [regroup_w(nc.scalar.copy, c + 1, g) for g in range(PASSES)]
-            for m in range(ROW_BLOCKS):
-                if c == 0:
-                    acc = first_accs[m]
-                    mx_passes(acc, c, m, [last])
-                else:
-                    acc = banks.tile([P, N_TILE], F32, tag="bank", name="acc")
-                    mx_passes(acc, c, m, range(PASSES))
-                result = out_stage.tile([P, N_TILE], F32)
-                nc.vector.tensor_tensor(
-                    out=result[:], in0=acc[:], in1=bias_all[:, n_cols], op=ALU.add
-                )
-                nc.sync.dma_start(out=out[m * P : (m + 1) * P, n_cols], in_=result[:])
-                if c + 1 < OUT_CHUNKS and m % 2 == 0:
-                    quantise_w(c + 1, m // 2, next_units[m // 2])
+        def scalar_ahead():
+            while counts[0] < len(scalar_units) and counts[1] < W_BUFS:
+                regroup_w(nc.scalar.copy, *scalar_units[counts[0]])
+                counts[0] = counts[0] + 1
+                counts[1] = counts[1] + 1
+
+        def quantise_scalar_unit(c, g):
+            quantise_w(c, g)
+            counts[1] = counts[1] - 1
+            scalar_ahead()
+
+        scalar_ahead()
+        mx_half(0, 0, last)
+
+        def tiles_of(half):
+            return range(half * TILES_PER_HALF, (half + 1) * TILES_PER_HALF)
+
+        quantise_w(1, 2)
+        mx_half(1, 0, 2)
+        quantise_scalar_unit(1, 3)
+        mx_half(1, 0, 3)
+        quantise_h(0, 1, h1[0])
+        for m in tiles_of(0):
+            finish(0, m)
+        open_tiles(0, 1)
+        for g in range(PASSES):
+            if g > 0:
+                quantise_h(g, 1, h1[g])
+            mx_half(0, 1, g)
+            finish(1, g)
+        open_tiles(1, 1)
+        for g in range(PASSES):
+            mx_half(1, 1, g)
+            finish(0, TILES_PER_HALF + g)
+            quantise_scalar_unit(2, g)
+        before = (1, 1)
+        for c in (2, 3):
+            for half in range(HALVES):
+                open_tiles(c, half)
+                if (c, half) == (3, 1):
+                    for k, m in enumerate(tiles_of(half)):
+                        for g in range(PASSES):
+                            mx_pass(c, m, g)
+                        finish(before[0], before[1] * TILES_PER_HALF + k)
+                    continue
+                for g in range(PASSES):
+                    mx_half(c, half, g)
+                    finish(before[0], before[1] * TILES_PER_HALF + g)
+                    if c == 2 and half == 1:
+                        quantise_scalar_unit(3, g)
+                before = (c, half)
+        for m in tiles_of(1):
+            finish(3, m)

@@ -157,13 +157,16 @@ def tile_customnetwork_pa_kernel(tc, h_lin, gamma, beta, w, b, out):
             )
             return x_t_block
 
-        def slopes_and_shifts(g):
+        def deviations(g):
             blocks = slice(g * PACK, (g + 1) * PACK)
-            beta_blocks = slice(FEATURE_BLOCKS + g * PACK, FEATURE_BLOCKS + (g + 1) * PACK)
             nc.scalar.activation(
                 out=std[:, blocks], in_=sum_sq[:, blocks], func=ACT.Sqrt,
                 bias=eps[:, 0:1], scale=1.0 / BATCH,
             )
+
+        def slopes_and_shifts(g):
+            blocks = slice(g * PACK, (g + 1) * PACK)
+            beta_blocks = slice(FEATURE_BLOCKS + g * PACK, FEATURE_BLOCKS + (g + 1) * PACK)
             nc.vector.reciprocal(out=rstd[:, blocks], in_=std[:, blocks])
             small.tensor_mul(
                 out=neg_mean_slope[:, blocks], in0=neg_mean_gamma[:, blocks], in1=rstd[:, blocks]
@@ -284,19 +287,17 @@ def tile_customnetwork_pa_kernel(tc, h_lin, gamma, beta, w, b, out):
             regroup_w(nc.vector.tensor_copy, 0, g)
         for g in (0, 1):
             quantise_w(0, g)
-        regroup_w(nc.vector.tensor_copy, 0, 2)
-        regroup_w_ring(False, 0, 3)
-        quantise_w(0, 2)
+        regroup_w_ring(False, 0, 2)
+        in_ring = [(0, 2), (0, 3), (1, 0), (1, 1), (1, 2)]
         mean_times_gamma(0)
-        in_ring = [(0, 3), (1, 0), (1, 1), (1, 2)]
         normed = [None] * PASSES
         for g in range(PASSES):
+            deviations(g)
             if g < last:
                 means(g + 1)
             slopes_and_shifts(g)
-            if g > 0:
-                quantise_w(*in_ring[g - 1])
-                regroup_w_ring(True, *in_ring[g])
+            quantise_w(*in_ring[g])
+            regroup_w_ring(True, *in_ring[g + 1])
             x_t_next = []
             if g < last:
                 x_t_next.append(transpose_and_square(g + 1, 0))
@@ -352,7 +353,8 @@ def tile_customnetwork_pa_kernel(tc, h_lin, gamma, beta, w, b, out):
             if g > 0:
                 quantise_h(g, 1, h1[g])
             mx_half(0, 1, g)
-            finish(1, g)
+        for m in tiles_of(0):
+            finish(1, m)
         open_tiles(1, 1)
         for g in range(PASSES):
             mx_half(1, 1, g)

@@ -90,10 +90,11 @@ def tile_customnetwork_pa_kernel(tc, h_lin, gamma, beta, w, b, out):
         load_w(0, 3)
         load_x(2)
         load_x(3)
-        nc.sync.dma_start(out=bias_all[:], in_=b.partition_broadcast(P))
         for c in range(1, OUT_CHUNKS):
             for g in range(PASSES):
                 load_w(c, g)
+            if c == 1:
+                nc.sync.dma_start(out=bias_all[:], in_=b.partition_broadcast(P))
 
         ident = const.tile([P, P], BF16)
         masks.make_identity(nc, ident[:])

@@ -15,7 +15,7 @@ P = 128
 PACK = 4
 K_PASS = P * PACK
 N_TILE = 512
-MEAN_COLS = 128
+MEAN_COLS = 64
 BN_EPS = 1e-5
 
 BATCH, D_IN, D_OUT = 1024, 2048, 2048
@@ -143,10 +143,12 @@ def tile_customnetwork_pa_kernel(tc, h_lin, gamma, beta, w, b, out):
             j = g * PACK + t
             x_t_block = banks.tile([P, BATCH], BF16, tag="bank", name="x_t")
             for r in range(ROW_BLOCKS):
-                nc.tensor.transpose(
-                    x_t_block[:, r * P : (r + 1) * P],
-                    x_sb[g][:, r, t * P : (t + 1) * P],
-                    ident[:],
+                nc.tensor.matmul(
+                    out=x_t_block[:, r * P : (r + 1) * P],
+                    lhsT=x_sb[g][:, r, t * P : (t + 1) * P],
+                    rhs=ident[:],
+                    start=True,
+                    stop=True,
                 )
             dropped = squares.tile([P, BATCH], BF16)
             nc.scalar.activation(

from contextlib import ExitStack

import concourse.masks as masks
import concourse.mybir as mybir

F32 = mybir.dt.float32
BF16 = mybir.dt.bfloat16
U32 = mybir.dt.uint32
U8 = mybir.dt.uint8
FP8X4 = mybir.dt.float8_e4m3fn_x4
ACT = mybir.ActivationFunctionType
ALU = mybir.AluOpType

P = 128
PACK = 4
K_PASS = P * PACK
N_TILE = 512
MEAN_COLS = 64
BN_EPS = 1e-5

BATCH, D_IN, D_OUT = 1024, 2048, 2048
FLOPS = 2 * BATCH * D_IN * D_OUT

ROW_BLOCKS = BATCH // P
PASSES = D_IN // K_PASS
FEATURE_BLOCKS = D_IN // P
OUT_CHUNKS = D_OUT // N_TILE
HALVES = 2
HALF_BATCH = BATCH // HALVES
HALF_PASSES = PASSES // HALVES
RUNS_PER_LOAD = 4


W_BUFS = 3


def tile_customnetwork_pa_kernel(tc, h_lin, gamma, beta, w, b, out):
    nc = tc.nc
    with ExitStack() as ctx:
        ctx.enter_context(tc.manual_schedule())
        const = ctx.enter_context(tc.tile_pool(name="const", bufs=1))
        keep = ctx.enter_context(tc.tile_pool(name="keep", bufs=1))
        wide = ctx.enter_context(tc.tile_pool(name="wide", bufs=6))
        squares = ctx.enter_context(tc.tile_pool(name="squares", bufs=1))
        h_pool = ctx.enter_context(tc.tile_pool(name="h_pool", bufs=2))
        h1_pool = ctx.enter_context(tc.tile_pool(name="h1_pool", bufs=4))
        w_pool = ctx.enter_context(tc.tile_pool(name="w_pool", bufs=W_BUFS))
        ring = ctx.enter_context(tc.tile_pool(name="ring", bufs=1))
        out_stage = ctx.enter_context(tc.tile_pool(name="out_stage", bufs=6))
        banks = ctx.enter_context(tc.psum_pool(name="banks", bufs=8))

        x_sb = [wide.tile([P, ROW_BLOCKS, K_PASS], BF16, tag="wide", name="x%d" % g) for g in range(PASSES)]
        w_raw = [
            [keep.tile([P, PACK, N_TILE], BF16, name="w_raw%d_%d" % (c, g)) for g in range(PASSES)]
            for c in range(OUT_CHUNKS)
        ]
        bias_all = const.tile([P, D_OUT], BF16)

        def load_x(g):
            columns = h_lin[:, g * K_PASS : (g + 1) * K_PASS].rearrange("(r p) d -> p r d", p=P)
            for r in range(0, ROW_BLOCKS, RUNS_PER_LOAD):
                nc.sync.dma_start(
                    out=x_sb[g][:, r : r + RUNS_PER_LOAD, :],
                    in_=columns[:, r : r + RUNS_PER_LOAD, :],
                )

        def load_w(c, g):
            nc.sync.dma_start(
                out=w_raw[c][g][:],
                in_=w[g * K_PASS : (g + 1) * K_PASS, c * N_TILE : (c + 1) * N_TILE].rearrange(
                    "(t p) n -> p t n", p=P
                ),
            )

        gb_rows = const.tile([P, P], BF16)
        nc.sync.dma_start(
            out=gb_rows[0:FEATURE_BLOCKS, :], in_=gamma.rearrange("(j p) -> j p", p=P)
        )
        nc.sync.dma_start(
            out=gb_rows[FEATURE_BLOCKS : 2 * FEATURE_BLOCKS, :],
            in_=beta.rearrange("(j p) -> j p", p=P),
        )
        nc.vector.memset(gb_rows[32:64, :], 0.0)
        nc.vector.memset(gb_rows[64:128, :], 0.0)
        load_x(0)
        load_w(0, 0)
        load_w(0, 1)
        load_x(1)
        load_w(0, 2)
        load_w(0, 3)
        load_x(2)
        load_x(3)
        for c in range(1, OUT_CHUNKS):
            for g in range(PASSES):
                load_w(c, g)
            if c == 1:
                nc.sync.dma_start(out=bias_all[:], in_=b.partition_broadcast(P))

        ident = const.tile([P, P], BF16)
        masks.make_identity(nc, ident[:])
        minus_inv_batch = const.tile([P, MEAN_COLS], BF16)
        nc.vector.memset(minus_inv_batch[:], -1.0 / BATCH)
        eps = const.tile([P, 1], F32)
        nc.vector.memset(eps[:], BN_EPS)
        table_warmer = const.tile([P, 1], F32)
        nc.scalar.activation(out=table_warmer[:], in_=eps[:], func=ACT.Sqrt)
        gb_ps = banks.tile([P, P], BF16, tag="bank")
        nc.tensor.transpose(gb_ps[:], gb_rows[:], ident[:])
        gb_cols = const.tile([P, 2 * FEATURE_BLOCKS], F32)
        nc.vector.tensor_copy(out=gb_cols[:], in_=gb_ps[:, 0 : 2 * FEATURE_BLOCKS])

        neg_mean = const.tile([P, FEATURE_BLOCKS], F32)
        sum_sq = const.tile([P, FEATURE_BLOCKS], F32)
        std = const.tile([P, FEATURE_BLOCKS], F32)
        rstd = const.tile([P, FEATURE_BLOCKS], F32)
        slope = const.tile([P, FEATURE_BLOCKS], F32)
        neg_mean_gamma = const.tile([P, FEATURE_BLOCKS], F32)
        neg_mean_slope = const.tile([P, FEATURE_BLOCKS], F32)
        shift = const.tile([P, FEATURE_BLOCKS], F32)
        small = nc.vector

        def means(g):
            neg_mean_ps = banks.tile([P, PACK, MEAN_COLS], F32, tag="bank")
            for t in range(PACK):
                for r in range(ROW_BLOCKS):
                    nc.tensor.matmul(
                        out=neg_mean_ps[:, t, :],
                        lhsT=x_sb[g][:, r, t * P : (t + 1) * P],
                        rhs=minus_inv_batch[:],
                        start=(r == 0),
                        stop=(r == ROW_BLOCKS - 1),
                    )
            blocks = slice(g * PACK, (g + 1) * PACK)
            nc.scalar.copy(out=neg_mean[:, blocks], in_=neg_mean_ps[:, :, 0])

        def mean_times_gamma(g):
            blocks = slice(g * PACK, (g + 1) * PACK)
            small.tensor_mul(
                out=neg_mean_gamma[:, blocks], in0=neg_mean[:, blocks], in1=gb_cols[:, blocks]
            )

        def transpose_and_square(g, t):
            j = g * PACK + t
            x_t_block = banks.tile([P, BATCH], BF16, tag="bank", name="x_t")
            for r in range(ROW_BLOCKS):
                nc.tensor.matmul(
                    out=x_t_block[:, r * P : (r + 1) * P],
                    lhsT=x_sb[g][:, r, t * P : (t + 1) * P],
                    rhs=ident[:],
                    start=True,
                    stop=True,
                )
            dropped = squares.tile([P, BATCH], BF16)
            nc.scalar.activation(
                out=dropped[:],
                in_=x_t_block[:],
                func=ACT.Square,
                bias=neg_mean[:, j : j + 1],
                accum_out=sum_sq[:, j : j + 1],
            )
            return x_t_block

        def deviations(g):
            blocks = slice(g * PACK, (g + 1) * PACK)
            nc.scalar.activation(
                out=std[:, blocks], in_=sum_sq[:, blocks], func=ACT.Sqrt,
                bias=eps[:, 0:1], scale=1.0 / BATCH,
            )

        def slopes_and_shifts(g):
            blocks = slice(g * PACK, (g + 1) * PACK)
            beta_blocks = slice(FEATURE_BLOCKS + g * PACK, FEATURE_BLOCKS + (g + 1) * PACK)
            nc.vector.reciprocal(out=rstd[:, blocks], in_=std[:, blocks])
            small.tensor_mul(
                out=neg_mean_slope[:, blocks], in0=neg_mean_gamma[:, blocks], in1=rstd[:, blocks]
            )
            small.tensor_mul(out=slope[:, blocks], in0=gb_cols[:, blocks], in1=rstd[:, blocks])
            small.tensor_add(
                out=shift[:, blocks], in0=neg_mean_slope[:, blocks], in1=gb_cols[:, beta_blocks]
            )

        def norm(g, x_t):
            normed = wide.tile([P, PACK, BATCH], BF16, tag="wide", name="normed%d" % g)
            for t in range(PACK):
                j = g * PACK + t
                nc.vector.tensor_scalar(
                    out=normed[:, t, :], in0=x_t[t][:],
                    scalar1=slope[:, j : j + 1], scalar2=shift[:, j : j + 1],
                    op0=ALU.mult, op1=ALU.add,
                )
            return normed

        h_codes = [[None] * HALVES for g in range(PASSES)]
        h_scales = [[None] * HALVES for g in range(PASSES)]

        def relu_regroup(on_scalar, normed, half):
            rows = slice(half * HALF_BATCH, (half + 1) * HALF_BATCH)
            pool = h1_pool if half else h_pool
            grouped = pool.tile([P, HALF_BATCH, PACK], BF16, align_bytes=64, tag="h_grouped")
            dst = grouped[:].rearrange("p (c i) t -> p c t i", i=4)
            src = normed[:, :, rows].rearrange("p t (c i) -> p c t i", i=4)
            if on_scalar:
                nc.scalar.activation(out=dst, in_=src, func=ACT.Relu)
            else:
                nc.vector.tensor_scalar_max(out=dst, in0=src, scalar1=0.0)
            return grouped

        def quantise_h(g, half, grouped):
            codes = keep.tile([P, HALF_BATCH], U32, name="h_codes%d_%d" % (g, half), align_bytes=64)
            scales = keep.tile([P, HALF_BATCH], U8, name="h_scales%d_%d" % (g, half), align_bytes=64)
            nc.vector.quantize_mx(
                out=codes[:].bitcast(FP8X4),
                scales=scales[:],
                in_=grouped[:].rearrange("p r t -> p (r t)"),
            )
            h_codes[g][half] = codes
            h_scales[g][half] = scales

        w_codes = [[None] * PASSES for c in range(OUT_CHUNKS)]
        w_scales = [[None] * PASSES for c in range(OUT_CHUNKS)]
        w_grouped = {}

        def regroup_w(copy_engine_op, c, g):
            grouped = w_pool.tile([P, N_TILE, PACK], BF16, align_bytes=64, tag="w_grouped")
            copy_engine_op(
                out=grouped[:].rearrange("p (c i) t -> p c t i", i=4),
                in_=w_raw[c][g][:].rearrange("p t (c i) -> p c t i", i=4),
            )
            w_grouped[(c, g)] = grouped

        def regroup_w_ring(on_gpsimd, c, g):
            grouped = ring.tile([P, N_TILE, PACK], BF16, align_bytes=64, tag="ring")
            dst = grouped[:].rearrange("p (c i) t -> p c t i", i=4)
            src = w_raw[c][g][:].rearrange("p t (c i) -> p c t i", i=4)
            if on_gpsimd:
                nc.gpsimd.tensor_scalar(
                    out=dst, in0=src, scalar1=1.0, scalar2=0.0, op0=ALU.mult, op1=ALU.add
                )
            else:
                nc.vector.tensor_copy(out=dst, in_=src)
            w_grouped[(c, g)] = grouped

        def quantise_w(c, g):
            codes = keep.tile([P, N_TILE], U32, name="w_codes%d_%d" % (c, g), align_bytes=64)
            scales = keep.tile([P, N_TILE], U8, name="w_scales%d_%d" % (c, g), align_bytes=64)
            nc.vector.quantize_mx(
                out=codes[:].bitcast(FP8X4),
                scales=scales[:],
                in_=w_grouped[(c, g)][:].rearrange("p n t -> p (n t)"),
            )
            w_codes[c][g] = codes
            w_scales[c][g] = scales

        TILES_PER_HALF = ROW_BLOCKS // HALVES
        accs = {}

        def open_tiles(c, half):
            for m in range(half * TILES_PER_HALF, (half + 1) * TILES_PER_HALF):
                accs[(c, m)] = banks.tile([P, N_TILE], F32, tag="bank", name="acc")

        def mx_pass(c, m, g):
            half = m // TILES_PER_HALF
            m_cols = slice((m % TILES_PER_HALF) * P, (m % TILES_PER_HALF + 1) * P)
            nc.tensor.matmul_mx(
                out=accs[(c, m)][:],
                lhsT=h_codes[g][half][:, m_cols].bitcast(FP8X4),
                lhsT_scale=h_scales[g][half][:, m_cols],
                rhs=w_codes[c][g][:].bitcast(FP8X4),
                rhs_scale=w_scales[c][g][:],
                start=(g == 0),
                stop=(g == PASSES - 1),
            )

        def mx_half(c, half, g):
            for m in range(half * TILES_PER_HALF, (half + 1) * TILES_PER_HALF):
                mx_pass(c, m, g)

        def finish(c, m):
            n_cols = slice(c * N_TILE, (c + 1) * N_TILE)
            result = out_stage.tile([P, N_TILE], F32, name="result")
            nc.vector.tensor_tensor(
                out=result[:], in0=accs[(c, m)][:], in1=bias_all[:, n_cols], op=ALU.add
            )
            nc.sync.dma_start(out=out[m * P : (m + 1) * P, n_cols], in_=result[:])

        last = PASSES - 1
        means(0)
        x_t = [transpose_and_square(0, t) for t in range(PACK)]
        for g in (0, 1):
            regroup_w(nc.vector.tensor_copy, 0, g)
        for g in (0, 1):
            quantise_w(0, g)
        regroup_w_ring(False, 0, 2)
        in_ring = [(0, 2), (0, 3), (1, 0), (1, 1), (1, 2)]
        mean_times_gamma(0)
        normed = [None] * PASSES
        for g in range(PASSES):
            deviations(g)
            if g < last:
                means(g + 1)
            slopes_and_shifts(g)
            quantise_w(*in_ring[g])
            regroup_w_ring(True, *in_ring[g + 1])
            x_t_next = []
            if g < last:
                x_t_next.append(transpose_and_square(g + 1, 0))
            normed[g] = norm(g, x_t)
            if g < last:
                for t in range(1, PACK):
                    x_t_next.append(transpose_and_square(g + 1, t))
            grouped = relu_regroup(False, normed[g], 0)
            if g < last:
                mean_times_gamma(g + 1)
            quantise_h(g, 0, grouped)
            x_t = x_t_next
            if g == last - 1:
                open_tiles(0, 0)
                for gg in range(last):
                    mx_half(0, 0, gg)
        open_tiles(1, 0)
        mx_half(1, 0, 0)
        mx_half(1, 0, 1)
        regroup_w(nc.scalar.copy, 1, 3)
        h1 = {}
        for g in range(PASSES):
            h1[g] = relu_regroup(True, normed[g], 1)
        scalar_units = [(c, g) for c in (2, 3) for g in range(PASSES)]
        counts = [0, 1]

        def scalar_ahead():
            while counts[0] < len(scalar_units) and counts[1] < W_BUFS:
                regroup_w(nc.scalar.copy, *scalar_units[counts[0]])
                counts[0] = counts[0] + 1
                counts[1] = counts[1] + 1

        def quantise_scalar_unit(c, g):
            quantise_w(c, g)
            counts[1] = counts[1] - 1
            scalar_ahead()

        scalar_ahead()
        mx_half(0, 0, last)

        def tiles_of(half):
            return range(half * TILES_PER_HALF, (half + 1) * TILES_PER_HALF)

        quantise_w(1, 2)
        mx_half(1, 0, 2)
        quantise_scalar_unit(1, 3)
        mx_half(1, 0, 3)
        quantise_h(0, 1, h1[0])
        for m in tiles_of(0):
            finish(0, m)
        open_tiles(0, 1)
        for g in range(PASSES):
            if g > 0:
                quantise_h(g, 1, h1[g])
            mx_half(0, 1, g)
        for m in tiles_of(0):
            finish(1, m)
        open_tiles(1, 1)
        for g in range(PASSES):
            mx_half(1, 1, g)
            finish(0, TILES_PER_HALF + g)
            quantise_scalar_unit(2, g)
        before = (1, 1)
        for c in (2, 3):
            for half in range(HALVES):
                open_tiles(c, half)
                if (c, half) == (3, 1):
                    for k, m in enumerate(tiles_of(half)):
                        for g in range(PASSES):
                            mx_pass(c, m, g)
                        finish(before[0], before[1] * TILES_PER_HALF + k)
                    continue
                for g in range(PASSES):
                    mx_half(c, half, g)
                    finish(before[0], before[1] * TILES_PER_HALF + g)
                    if c == 2 and half == 1:
                        quantise_scalar_unit(3, g)
                before = (c, half)
        for m in tiles_of(1):
            finish(3, m)
